import numpy as np
import ml_dtypes


def mxq(x, axis, fmt="e4m3"):
    dtype, down = {"e4m3": (ml_dtypes.float8_e4m3fn, 7), "e5m2": (ml_dtypes.float8_e5m2, 14)}[fmt]
    v = np.moveaxis(np.asarray(x, np.float32).astype(ml_dtypes.bfloat16).astype(np.float64), axis, -1)
    blocks = v.reshape(v.shape[:-1] + (-1, 32))
    amax = np.abs(blocks).max(-1, keepdims=True)
    byte = np.maximum(np.where(amax > 0, np.frexp(amax)[1] - 1 + 127, 0) - down, 1)
    scale = np.exp2(byte - 127.0)
    codes = (blocks / scale).astype(np.float32).astype(dtype).astype(np.float64)
    return np.moveaxis((codes * scale).reshape(v.shape), -1, axis)


WIDE = False


def mx_kscale(k):
    if not WIDE:
        return np.ones(k)
    levels = np.array([10, -10, 5, -5, 0])
    a = np.random.permutation(np.resize(levels, k // 512 * 4)).reshape(k // 512, 4)
    idx = np.arange(k)
    return np.exp2(a[idx // 512, idx % 128 // 32])


BF16 = ml_dtypes.bfloat16


def bf(x):
    return np.asarray(x, np.float32).astype(BF16)


def f64(x):
    return np.asarray(x).astype(np.float64)


L, R, T, H, F = 4, 4, 256, 1024, 1024


def setup_inputs():
    s, t = mx_kscale(H), mx_kscale(F)
    return {"x": bf(np.random.standard_normal((R, T, H)) * s),
            "w_first": bf(np.random.standard_normal((R, H, F)) / np.sqrt(R * H) / s[:, None] * t),
            "w_second": bf(np.random.standard_normal((R, F, H)) / np.sqrt(R * F) / t[:, None])}


def reference(x, w_first, w_second):
    y = mxq(f64(x), 2, "e4m3") @ mxq(f64(w_first), 1, "e4m3")
    reduced = y.sum(0)
    z = mxq(reduced, 1, "e4m3")[None] @ mxq(f64(w_second), 1, "e4m3")
    total = z.sum(0)
    return np.broadcast_to(total[None], z.shape).copy()

@@ -1,0 +1,222 @@
+from contextlib import ExitStack
+
+import concourse.mybir as mybir
+from concourse.masks import make_identity
+
+F32 = mybir.dt.float32
+BF16 = mybir.dt.bfloat16
+U32 = mybir.dt.uint32
+U8 = mybir.dt.uint8
+FP8X4 = mybir.dt.float8_e4m3fn_x4
+
+P = 128
+PACK = 4
+K_PASS = P * PACK
+R, T, H, F = 4, 256, 1024, 1024
+W = 1024
+N_CHUNKS = 16
+RAW_BUFS = 8
+GRP_BUFS = 4
+CODE_BUFS = 6
+V_COLS = 496
+
+FLOPS = 2 * 2 * R * T * H * F
+
+
+def tile_multilayerallreduce_pa_kernel(tc, x, w_first, w_second, out):
+    nc = tc.nc
+    with ExitStack() as ctx:
+        const = ctx.enter_context(tc.tile_pool(name="const", bufs=1))
+        keep = ctx.enter_context(tc.tile_pool(name="keep", bufs=1))
+        rawp = ctx.enter_context(tc.tile_pool(name="rawp", bufs=RAW_BUFS))
+        grpp = ctx.enter_context(tc.tile_pool(name="grpp", bufs=GRP_BUFS))
+        codp = ctx.enter_context(tc.tile_pool(name="codp", bufs=CODE_BUFS))
+        psum = ctx.enter_context(tc.psum_pool(name="psum", bufs=1))
+        ctx.enter_context(tc.manual_schedule())
+
+        raw = {}
+        grp = {}
+        codes = {}
+        scales = {}
+
+        xraw = []
+        for r in range(R):
+            xr = keep.tile([P, 2, H], BF16, name="xraw%d" % r)
+            nc.sync.dma_start(out=xr[:], in_=x[r].rearrange("(p tt) h -> p tt h", tt=2))
+            xraw.append(xr)
+
+        def load_w(c):
+            r, g = (c % 8) // 2, c % 2
+            t = rawp.tile([P, PACK, W], BF16, name="raw%d" % c, tag="raw")
+            if c < 8:
+                src = w_first[r, g * K_PASS : (g + 1) * K_PASS, :].rearrange("(p j) f -> p j f", j=PACK)
+            else:
+                src = w_second[r, g * K_PASS : (g + 1) * K_PASS, :].rearrange("(j p) f -> p j f", p=P)
+            nc.sync.dma_start(out=t[:], in_=src)
+            raw[c] = t
+
+        for c in range(RAW_BUFS):
+            load_w(c)
+
+        ident = const.tile([P, P], F32, name="ident")
+        make_identity(nc, ident[:])
+
+        xcodes = []
+        xscales = []
+        xgrp = []
+        for r in range(R):
+            xw = xraw[r][:].bitcast(F32)
+            gx = keep.tile([P, 2, T, 2], F32, name="gx%d" % r, align_bytes=64)
+            for g in range(2):
+                xt = psum.tile([P, 2, T], F32, name="xt%d_%d" % (r, g), tag="bank%d" % (2 * r + g))
+                for u in range(2):
+                    for tt in range(2):
+                        nc.tensor.transpose(
+                            xt[:, u, tt * P : (tt + 1) * P],
+                            xw[:, tt, 256 * g + u : 256 * (g + 1) : 2],
+                            ident[:],
+                        )
+                eng_copy = nc.vector.tensor_copy if g == 0 else nc.scalar.copy
+                eng_copy(out=gx[:, g, :, :], in_=xt[:].rearrange("p u c -> p c u"))
+            xgrp.append(gx)
+
+        def quant_x(r):
+            xc = keep.tile([P, 2 * T], U32, name="xc%d" % r, align_bytes=64)
+            xs = keep.tile([P, 2 * T], U8, name="xs%d" % r, align_bytes=64)
+            nc.vector.quantize_mx(
+                out=xc[:].bitcast(FP8X4),
+                scales=xs[:],
+                in_=xgrp[r][:].rearrange("p g c u -> p (g c u)").bitcast(BF16),
+            )
+            xcodes.append(xc)
+            xscales.append(xs)
+
+        for r in range(R):
+            quant_x(r)
+
+        def regroup(c):
+            g = grpp.tile([P, W, PACK], BF16, name="grp%d" % c, tag="grp", align_bytes=64)
+            a = V_COLS
+            nc.vector.tensor_copy(
+                out=g[:, 0:a, :].rearrange("p (c i) t -> p c t i", i=4),
+                in_=raw[c][:, :, 0:a].rearrange("p t (c i) -> p c t i", i=4),
+            )
+            nc.scalar.copy(
+                out=g[:, a:W, :].rearrange("p (c i) t -> p c t i", i=4),
+                in_=raw[c][:, :, a:W].rearrange("p t (c i) -> p c t i", i=4),
+            )
+            grp[c] = g
+
+        def quant(c):
+            cd = codp.tile([P, W], U32, name="codes%d" % c, tag="codes", align_bytes=64)
+            sc = codp.tile([P, W], U8, name="scales%d" % c, tag="scales", align_bytes=64)
+            nc.vector.quantize_mx(
+                out=cd[:].bitcast(FP8X4),
+                scales=sc[:],
+                in_=grp[c][:].rearrange("p w t -> p (w t)"),
+            )
+            codes[c] = cd
+            scales[c] = sc
+
+        y = []
+        o = {}
+
+        def mm1(c):
+            r, g = c // 2, c % 2
+            if c == 0:
+                for m in range(8):
+                    y.append(psum.tile([P, T], F32, name="y%d" % m, tag="bank%d" % m))
+            for m in range(8):
+                nc.tensor.matmul_mx(
+                    out=y[m][:],
+                    lhsT=codes[c][:, m * P : (m + 1) * P].bitcast(FP8X4),
+                    lhsT_scale=scales[c][:, m * P : (m + 1) * P],
+                    rhs=xcodes[r][:, g * T : (g + 1) * T].bitcast(FP8X4),
+                    rhs_scale=xscales[r][:, g * T : (g + 1) * T],
+                    start=(c == 0),
+                    stop=(c == 7),
+                )
+
+        red = []
+        g2 = []
+        c2 = []
+        s2 = []
+
+        def evac_red():
+            for g in range(2):
+                rp = keep.tile([P, PACK, T], BF16, name="red%d" % g)
+                for t in range(PACK):
+                    eng_copy = nc.vector.tensor_copy if g == 0 else nc.scalar.copy
+                    eng_copy(out=rp[:, t, :], in_=y[PACK * g + t][:])
+                red.append(rp)
+
+        def regroup_red():
+            for g in range(2):
+                gg = keep.tile([P, T, PACK], BF16, name="g2_%d" % g, align_bytes=64)
+                nc.vector.tensor_copy(
+                    out=gg[:].rearrange("p (c i) t -> p c t i", i=4),
+                    in_=red[g][:].rearrange("p t (c i) -> p c t i", i=4),
+                )
+                g2.append(gg)
+
+        def quant_red():
+            for g in range(2):
+                cd = keep.tile([P, T], U32, name="c2_%d" % g, align_bytes=64)
+                sc = keep.tile([P, T], U8, name="s2_%d" % g, align_bytes=64)
+                nc.vector.quantize_mx(
+                    out=cd[:].bitcast(FP8X4),
+                    scales=sc[:],
+                    in_=g2[g][:].rearrange("p w t -> p (w t)"),
+                )
+                c2.append(cd)
+                s2.append(sc)
+
+        def mm2(c):
+            g = c % 2
+            if c == 8:
+                for tt in range(2):
+                    for n in range(2):
+                        o[(tt, n)] = psum.tile([P, 512], F32, name="o%d_%d" % (tt, n), tag="bank%d" % (2 * tt + n))
+            for tt in range(2):
+                for n in range(2):
+                    nc.tensor.matmul_mx(
+                        out=o[(tt, n)][:],
+                        lhsT=c2[g][:, tt * P : (tt + 1) * P].bitcast(FP8X4),
+                        lhsT_scale=s2[g][:, tt * P : (tt + 1) * P],
+                        rhs=codes[c][:, n * 512 : (n + 1) * 512].bitcast(FP8X4),
+                        rhs_scale=scales[c][:, n * 512 : (n + 1) * 512],
+                        start=(c == 8),
+                        stop=(c == 15),
+                    )
+
+        pending = []
+        red_ready = False
+        for i in range(N_CHUNKS + 1):
+            if i < N_CHUNKS:
+                regroup(i)
+                if i + RAW_BUFS < N_CHUNKS:
+                    load_w(i + RAW_BUFS)
+            if i >= 1:
+                quant(i - 1)
+                if i - 1 < 8:
+                    mm1(i - 1)
+                else:
+                    pending.append(i - 1)
+            if i == 9:
+                evac_red()
+            if i == 10:
+                regroup_red()
+            if i == 11:
+                quant_red()
+                red_ready = True
+            if red_ready:
+                for c in pending:
+                    mm2(c)
+                pending = []
+
+        for tt in range(2):
+            ot = keep.tile([P, H], F32, name="ot%d" % tt)
+            nc.vector.tensor_copy(out=ot[:, 0:512], in_=o[(tt, 0)][:])
+            nc.scalar.copy(out=ot[:, 512:1024], in_=o[(tt, 1)][:])
+            for r in range(R):
+                nc.sync.dma_start(out=out[r].rearrange("(p tt) h -> p tt h", tt=2)[:, tt, :], in_=ot[:])

@@ -15,10 +15,15 @@ K_PASS = P * PACK
 R, T, H, F = 4, 256, 1024, 1024
 W = 1024
 N_CHUNKS = 16
+LAST = N_CHUNKS - 1
+Q_COLS = 256
 RAW_BUFS = 8
 GRP_BUFS = 4
 CODE_BUFS = 6
-V_COLS = 496
+LATE = 5
+PERM = 0
+X_AFTER = 1
+RED_AT = 9
 
 FLOPS = 2 * 2 * R * T * H * F
 
@@ -34,13 +39,24 @@ def tile_multilayerallreduce_pa_kernel(tc, x, w_first, w_second, out):
         psum = ctx.enter_context(tc.psum_pool(name="psum", bufs=1))
         ctx.enter_context(tc.manual_schedule())
 
+        late = list(range(N_CHUNKS - LATE, N_CHUNKS))
+        items = [((c, 0, W // 2), (c, W // 2, W // 2)) for c in range(N_CHUNKS - LATE)]
+        items += [((c, 0, Q_COLS), (c, Q_COLS, Q_COLS)) for c in late]
+        right = [(c, q * Q_COLS, Q_COLS) for q in (2, 3) for c in late]
+        items += [(right[k], right[k + 1]) for k in range(0, len(right), 2)]
+        n_items = len(items)
+
+        def closed_by(i):
+            return [col0 // Q_COLS for c, col0, cols in items[i] if c == LAST]
+
         raw = {}
         grp = {}
         codes = {}
         scales = {}
 
         xraw = []
-        for r in range(R):
+
+        def load_x(r):
             xr = keep.tile([P, 2, H], BF16, name="xraw%d" % r)
             nc.sync.dma_start(out=xr[:], in_=x[r].rearrange("(p tt) h -> p tt h", tt=2))
             xraw.append(xr)
@@ -48,14 +64,18 @@ def tile_multilayerallreduce_pa_kernel(tc, x, w_first, w_second, out):
         def load_w(c):
             r, g = (c % 8) // 2, c % 2
             t = rawp.tile([P, PACK, W], BF16, name="raw%d" % c, tag="raw")
-            if c < 8:
-                src = w_first[r, g * K_PASS : (g + 1) * K_PASS, :].rearrange("(p j) f -> p j f", j=PACK)
+            rows = (w_first if c < 8 else w_second)[r, g * K_PASS : (g + 1) * K_PASS, :]
+            if c < 8 or PERM:
+                nc.sync.dma_start(out=t[:], in_=rows.rearrange("(p j) f -> p j f", j=PACK))
             else:
-                src = w_second[r, g * K_PASS : (g + 1) * K_PASS, :].rearrange("(j p) f -> p j f", p=P)
-            nc.sync.dma_start(out=t[:], in_=src)
+                nc.sync.dma_start(out=t[:], in_=rows.rearrange("(j p) f -> p j f", p=P))
             raw[c] = t
 
-        for c in range(RAW_BUFS):
+        for c in range(X_AFTER + 1):
+            load_w(c)
+        for r in range(R):
+            load_x(r)
+        for c in range(X_AFTER + 1, RAW_BUFS):
             load_w(c)
 
         ident = const.tile([P, P], F32, name="ident")
@@ -64,7 +84,8 @@ def tile_multilayerallreduce_pa_kernel(tc, x, w_first, w_second, out):
         xcodes = []
         xscales = []
         xgrp = []
-        for r in range(R):
+
+        def transpose_x(r):
             xw = xraw[r][:].bitcast(F32)
             gx = keep.tile([P, 2, T, 2], F32, name="gx%d" % r, align_bytes=64)
             for g in range(2):
@@ -91,37 +112,28 @@ def tile_multilayerallreduce_pa_kernel(tc, x, w_first, w_second, out):
             xcodes.append(xc)
             xscales.append(xs)
 
-        for r in range(R):
-            quant_x(r)
-
-        def regroup(c):
-            g = grpp.tile([P, W, PACK], BF16, name="grp%d" % c, tag="grp", align_bytes=64)
-            a = V_COLS
-            nc.vector.tensor_copy(
-                out=g[:, 0:a, :].rearrange("p (c i) t -> p c t i", i=4),
-                in_=raw[c][:, :, 0:a].rearrange("p t (c i) -> p c t i", i=4),
-            )
-            nc.scalar.copy(
-                out=g[:, a:W, :].rearrange("p (c i) t -> p c t i", i=4),
-                in_=raw[c][:, :, a:W].rearrange("p t (c i) -> p c t i", i=4),
-            )
-            grp[c] = g
-
-        def quant(c):
-            cd = codp.tile([P, W], U32, name="codes%d" % c, tag="codes", align_bytes=64)
-            sc = codp.tile([P, W], U8, name="scales%d" % c, tag="scales", align_bytes=64)
-            nc.vector.quantize_mx(
-                out=cd[:].bitcast(FP8X4),
-                scales=sc[:],
-                in_=grp[c][:].rearrange("p w t -> p (w t)"),
-            )
-            codes[c] = cd
-            scales[c] = sc
+        def regroup(i):
+            cols = items[i][0][2]
+            g = grpp.tile([P, 2 * cols, PACK], BF16, name="grp%d" % i, tag="grp%d" % cols, align_bytes=64)
+            for s, eng_copy in enumerate((nc.vector.tensor_copy, nc.scalar.copy)):
+                c, col0, cols = items[i][s]
+                dst = g[:, s * cols : (s + 1) * cols, :]
+                if PERM and c < 8:
+                    dst = dst.rearrange("p (i q) t -> p q t i", i=4)
+                else:
+                    dst = dst.rearrange("p (q i) t -> p q t i", i=4)
+                eng_copy(out=dst, in_=raw[c][:, :, col0 : col0 + cols].rearrange("p t (q i) -> p q t i", i=4))
+            grp[i] = g
 
         y = []
         o = {}
+        red = []
+        g2 = []
+        c2 = []
+        s2 = []
 
-        def mm1(c):
+        def mm1(i):
+            c = items[i][0][0]
             r, g = c // 2, c % 2
             if c == 0:
                 for m in range(8):
@@ -129,33 +141,74 @@ def tile_multilayerallreduce_pa_kernel(tc, x, w_first, w_second, out):
             for m in range(8):
                 nc.tensor.matmul_mx(
                     out=y[m][:],
-                    lhsT=codes[c][:, m * P : (m + 1) * P].bitcast(FP8X4),
-                    lhsT_scale=scales[c][:, m * P : (m + 1) * P],
+                    lhsT=codes[i][:, m * P : (m + 1) * P].bitcast(FP8X4),
+                    lhsT_scale=scales[i][:, m * P : (m + 1) * P],
                     rhs=xcodes[r][:, g * T : (g + 1) * T].bitcast(FP8X4),
                     rhs_scale=xscales[r][:, g * T : (g + 1) * T],
                     start=(c == 0),
                     stop=(c == 7),
                 )
 
-        red = []
-        g2 = []
-        c2 = []
-        s2 = []
+        def mm2(i):
+            if not o:
+                for tt in range(2):
+                    for q in range(W // Q_COLS):
+                        o[(tt, q)] = psum.tile([P, Q_COLS], F32, name="o%d_%d" % (tt, q), tag="bank%d" % (2 * q + tt))
+            for s in range(2):
+                c, col0, cols = items[i][s]
+                for tt in range(2):
+                    for k in range(cols // Q_COLS):
+                        at = s * cols + k * Q_COLS
+                        nc.tensor.matmul_mx(
+                            out=o[(tt, col0 // Q_COLS + k)][:],
+                            lhsT=c2[c % 2][:, tt * P : (tt + 1) * P].bitcast(FP8X4),
+                            lhsT_scale=s2[c % 2][:, tt * P : (tt + 1) * P],
+                            rhs=codes[i][:, at : at + Q_COLS].bitcast(FP8X4),
+                            rhs_scale=scales[i][:, at : at + Q_COLS],
+                            start=(c == 8),
+                            stop=(c == LAST),
+                        )
+
+        waiting = []
+        multiplied = set()
+
+        def multiply_what_is_ready():
+            for i in waiting:
+                first_layer = items[i][0][0] < 8
+                ready = len(xcodes) == R if first_layer else len(c2) == 2
+                if ready and i not in multiplied:
+                    (mm1 if first_layer else mm2)(i)
+                    multiplied.add(i)
+
+        def quant(i):
+            if i < 0 or i in codes:
+                return
+            width = 2 * items[i][0][2]
+            cd = codp.tile([P, width], U32, name="codes%d" % i, tag="codes%d" % width, align_bytes=64)
+            sc = codp.tile([P, width], U8, name="scales%d" % i, tag="scales%d" % width, align_bytes=64)
+            nc.vector.quantize_mx(
+                out=cd[:].bitcast(FP8X4),
+                scales=sc[:],
+                in_=grp[i][:].rearrange("p w t -> p (w t)"),
+            )
+            codes[i] = cd
+            scales[i] = sc
+            waiting.append(i)
+            multiply_what_is_ready()
 
         def evac_red():
             for g in range(2):
                 rp = keep.tile([P, PACK, T], BF16, name="red%d" % g)
                 for t in range(PACK):
-                    eng_copy = nc.vector.tensor_copy if g == 0 else nc.scalar.copy
-                    eng_copy(out=rp[:, t, :], in_=y[PACK * g + t][:])
+                    nc.scalar.copy(out=rp[:, t, :], in_=y[PACK * g + t][:])
                 red.append(rp)
 
         def regroup_red():
             for g in range(2):
                 gg = keep.tile([P, T, PACK], BF16, name="g2_%d" % g, align_bytes=64)
                 nc.vector.tensor_copy(
-                    out=gg[:].rearrange("p (c i) t -> p c t i", i=4),
-                    in_=red[g][:].rearrange("p t (c i) -> p c t i", i=4),
+                    out=gg[:].rearrange("p (q i) t -> p q t i", i=4),
+                    in_=red[g][:].rearrange("p t (q i) -> p q t i", i=4),
                 )
                 g2.append(gg)
 
@@ -170,53 +223,42 @@ def tile_multilayerallreduce_pa_kernel(tc, x, w_first, w_second, out):
                 )
                 c2.append(cd)
                 s2.append(sc)
+            multiply_what_is_ready()
 
-        def mm2(c):
-            g = c % 2
-            if c == 8:
-                for tt in range(2):
-                    for n in range(2):
-                        o[(tt, n)] = psum.tile([P, 512], F32, name="o%d_%d" % (tt, n), tag="bank%d" % (2 * tt + n))
-            for tt in range(2):
-                for n in range(2):
-                    nc.tensor.matmul_mx(
-                        out=o[(tt, n)][:],
-                        lhsT=c2[g][:, tt * P : (tt + 1) * P].bitcast(FP8X4),
-                        lhsT_scale=s2[g][:, tt * P : (tt + 1) * P],
-                        rhs=codes[c][:, n * 512 : (n + 1) * 512].bitcast(FP8X4),
-                        rhs_scale=scales[c][:, n * 512 : (n + 1) * 512],
-                        start=(c == 8),
-                        stop=(c == 15),
-                    )
-
-        pending = []
-        red_ready = False
-        for i in range(N_CHUNKS + 1):
-            if i < N_CHUNKS:
-                regroup(i)
-                if i + RAW_BUFS < N_CHUNKS:
-                    load_w(i + RAW_BUFS)
-            if i >= 1:
-                quant(i - 1)
-                if i - 1 < 8:
-                    mm1(i - 1)
-                else:
-                    pending.append(i - 1)
-            if i == 9:
-                evac_red()
-            if i == 10:
-                regroup_red()
-            if i == 11:
-                quant_red()
-                red_ready = True
-            if red_ready:
-                for c in pending:
-                    mm2(c)
-                pending = []
-
-        for tt in range(2):
-            ot = keep.tile([P, H], F32, name="ot%d" % tt)
-            nc.vector.tensor_copy(out=ot[:, 0:512], in_=o[(tt, 0)][:])
-            nc.scalar.copy(out=ot[:, 512:1024], in_=o[(tt, 1)][:])
+        def evac_out(quarters):
+            n = len(quarters)
+            ot = keep.tile([P, 2, n * Q_COLS], F32, name="ot%d" % quarters[0])
+            for k, q in enumerate(quarters):
+                nc.vector.tensor_copy(out=ot[:, 0, k * Q_COLS : (k + 1) * Q_COLS], in_=o[(0, q)][:])
+                nc.scalar.copy(out=ot[:, 1, k * Q_COLS : (k + 1) * Q_COLS], in_=o[(1, q)][:])
             for r in range(R):
-                nc.sync.dma_start(out=out[r].rearrange("(p tt) h -> p tt h", tt=2)[:, tt, :], in_=ot[:])
+                nc.sync.dma_start(
+                    out=out[r].rearrange("(p tt) h -> p tt h", tt=2)[:, :, quarters[0] * Q_COLS : (quarters[0] + n) * Q_COLS],
+                    in_=ot[:],
+                )
+
+        for i in range(n_items):
+            if closed_by(i):
+                quant(i - 1)
+            regroup(i)
+            if i + RAW_BUFS < N_CHUNKS:
+                load_w(i + RAW_BUFS)
+            if i == RED_AT + 1:
+                regroup_red()
+            if i >= 1 and closed_by(i - 1):
+                evac_out(closed_by(i - 1))
+            quant(i - 1)
+            if closed_by(i):
+                quant(i)
+            if i == X_AFTER:
+                for r in range(R):
+                    transpose_x(r)
+                    if r >= 1:
+                        quant_x(r - 1)
+                quant_x(R - 1)
+                multiply_what_is_ready()
+            if i == RED_AT:
+                evac_red()
+            if i == RED_AT + 1:
+                quant_red()
+        evac_out(closed_by(n_items - 1))

@@ -21,7 +21,7 @@ RAW_BUFS = 8
 GRP_BUFS = 4
 CODE_BUFS = 6
 LATE = 5
-PERM = 0
+PERM = 1
 X_AFTER = 1
 RED_AT = 9
 

@@ -21,9 +21,10 @@ RAW_BUFS = 8
 GRP_BUFS = 4
 CODE_BUFS = 6
 LATE = 5
-PERM = 1
 X_AFTER = 1
 RED_AT = 9
+EV_LAG = 2
+XV = ()
 
 FLOPS = 2 * 2 * R * T * H * F
 
@@ -39,15 +40,28 @@ def tile_multilayerallreduce_pa_kernel(tc, x, w_first, w_second, out):
         psum = ctx.enter_context(tc.psum_pool(name="psum", bufs=1))
         ctx.enter_context(tc.manual_schedule())
 
-        late = list(range(N_CHUNKS - LATE, N_CHUNKS))
-        items = [((c, 0, W // 2), (c, W // 2, W // 2)) for c in range(N_CHUNKS - LATE)]
-        items += [((c, 0, Q_COLS), (c, Q_COLS, Q_COLS)) for c in late]
-        right = [(c, q * Q_COLS, Q_COLS) for q in (2, 3) for c in late]
-        items += [(right[k], right[k + 1]) for k in range(0, len(right), 2)]
+        late = list(range(N_CHUNKS - LATE, LAST))
+        items = [[(c, 0, W)] for c in range(N_CHUNKS - LATE)]
+        items += [[(c, 0, W // 2)] for c in late + [LAST]]
+        for q in (2, 3):
+            items += [[(late[k], q * Q_COLS, Q_COLS), (late[k + 1], q * Q_COLS, Q_COLS)] for k in range(0, len(late), 2)]
+            items.append([(LAST, q * Q_COLS, Q_COLS)])
         n_items = len(items)
 
+        def width(i):
+            return sum(cols for c, col0, cols in items[i])
+
+        def shares(i):
+            if len(items[i]) == 2:
+                return items[i]
+            c, col0, cols = items[i][0]
+            return [(c, col0, cols // 2), (c, col0 + cols // 2, cols // 2)]
+
         def closed_by(i):
-            return [col0 // Q_COLS for c, col0, cols in items[i] if c == LAST]
+            if i < 0 or items[i][0][0] != LAST:
+                return []
+            c, col0, cols = items[i][0]
+            return list(range(col0 // Q_COLS, (col0 + cols) // Q_COLS))
 
         raw = {}
         grp = {}
@@ -65,10 +79,7 @@ def tile_multilayerallreduce_pa_kernel(tc, x, w_first, w_second, out):
             r, g = (c % 8) // 2, c % 2
             t = rawp.tile([P, PACK, W], BF16, name="raw%d" % c, tag="raw")
             rows = (w_first if c < 8 else w_second)[r, g * K_PASS : (g + 1) * K_PASS, :]
-            if c < 8 or PERM:
-                nc.sync.dma_start(out=t[:], in_=rows.rearrange("(p j) f -> p j f", j=PACK))
-            else:
-                nc.sync.dma_start(out=t[:], in_=rows.rearrange("(j p) f -> p j f", p=P))
+            nc.sync.dma_start(out=t[:], in_=rows.rearrange("(p j) f -> p j f", j=PACK))
             raw[c] = t
 
         for c in range(X_AFTER + 1):
@@ -97,7 +108,7 @@ def tile_multilayerallreduce_pa_kernel(tc, x, w_first, w_second, out):
                             xw[:, tt, 256 * g + u : 256 * (g + 1) : 2],
                             ident[:],
                         )
-                eng_copy = nc.vector.tensor_copy if g == 0 else nc.scalar.copy
+                eng_copy = nc.vector.tensor_copy if 2 * r + g in XV else nc.scalar.copy
                 eng_copy(out=gx[:, g, :, :], in_=xt[:].rearrange("p u c -> p c u"))
             xgrp.append(gx)
 
@@ -113,16 +124,16 @@ def tile_multilayerallreduce_pa_kernel(tc, x, w_first, w_second, out):
             xscales.append(xs)
 
         def regroup(i):
-            cols = items[i][0][2]
-            g = grpp.tile([P, 2 * cols, PACK], BF16, name="grp%d" % i, tag="grp%d" % cols, align_bytes=64)
-            for s, eng_copy in enumerate((nc.vector.tensor_copy, nc.scalar.copy)):
-                c, col0, cols = items[i][s]
-                dst = g[:, s * cols : (s + 1) * cols, :]
-                if PERM and c < 8:
+            g = grpp.tile([P, width(i), PACK], BF16, name="grp%d" % i, tag="grp%d" % width(i), align_bytes=64)
+            at = 0
+            for (c, col0, cols), eng_copy in zip(shares(i), (nc.vector.tensor_copy, nc.scalar.copy)):
+                dst = g[:, at : at + cols, :]
+                if c < 8:
                     dst = dst.rearrange("p (i q) t -> p q t i", i=4)
                 else:
                     dst = dst.rearrange("p (q i) t -> p q t i", i=4)
                 eng_copy(out=dst, in_=raw[c][:, :, col0 : col0 + cols].rearrange("p t (q i) -> p q t i", i=4))
+                at += cols
             grp[i] = g
 
         y = []
@@ -154,20 +165,20 @@ def tile_multilayerallreduce_pa_kernel(tc, x, w_first, w_second, out):
                 for tt in range(2):
                     for q in range(W // Q_COLS):
                         o[(tt, q)] = psum.tile([P, Q_COLS], F32, name="o%d_%d" % (tt, q), tag="bank%d" % (2 * q + tt))
-            for s in range(2):
-                c, col0, cols = items[i][s]
+            at = 0
+            for c, col0, cols in items[i]:
                 for tt in range(2):
                     for k in range(cols // Q_COLS):
-                        at = s * cols + k * Q_COLS
                         nc.tensor.matmul_mx(
                             out=o[(tt, col0 // Q_COLS + k)][:],
                             lhsT=c2[c % 2][:, tt * P : (tt + 1) * P].bitcast(FP8X4),
                             lhsT_scale=s2[c % 2][:, tt * P : (tt + 1) * P],
-                            rhs=codes[i][:, at : at + Q_COLS].bitcast(FP8X4),
-                            rhs_scale=scales[i][:, at : at + Q_COLS],
+                            rhs=codes[i][:, at + k * Q_COLS : at + (k + 1) * Q_COLS].bitcast(FP8X4),
+                            rhs_scale=scales[i][:, at + k * Q_COLS : at + (k + 1) * Q_COLS],
                             start=(c == 8),
                             stop=(c == LAST),
                         )
+                at += cols
 
         waiting = []
         multiplied = set()
@@ -183,9 +194,8 @@ def tile_multilayerallreduce_pa_kernel(tc, x, w_first, w_second, out):
         def quant(i):
             if i < 0 or i in codes:
                 return
-            width = 2 * items[i][0][2]
-            cd = codp.tile([P, width], U32, name="codes%d" % i, tag="codes%d" % width, align_bytes=64)
-            sc = codp.tile([P, width], U8, name="scales%d" % i, tag="scales%d" % width, align_bytes=64)
+            cd = codp.tile([P, width(i)], U32, name="codes%d" % i, tag="codes%d" % width(i), align_bytes=64)
+            sc = codp.tile([P, width(i)], U8, name="scales%d" % i, tag="scales%d" % width(i), align_bytes=64)
             nc.vector.quantize_mx(
                 out=cd[:].bitcast(FP8X4),
                 scales=sc[:],
@@ -226,6 +236,8 @@ def tile_multilayerallreduce_pa_kernel(tc, x, w_first, w_second, out):
             multiply_what_is_ready()
 
         def evac_out(quarters):
+            if not quarters:
+                return
             n = len(quarters)
             ot = keep.tile([P, 2, n * Q_COLS], F32, name="ot%d" % quarters[0])
             for k, q in enumerate(quarters):
@@ -238,19 +250,17 @@ def tile_multilayerallreduce_pa_kernel(tc, x, w_first, w_second, out):
                 )
 
         for i in range(n_items):
-            if closed_by(i):
-                quant(i - 1)
             regroup(i)
             if i + RAW_BUFS < N_CHUNKS:
                 load_w(i + RAW_BUFS)
             if i == RED_AT + 1:
                 regroup_red()
-            if i >= 1 and closed_by(i - 1):
-                evac_out(closed_by(i - 1))
+            evac_out(closed_by(i - EV_LAG))
             quant(i - 1)
             if closed_by(i):
                 quant(i)
             if i == X_AFTER:
+                quant(i)
                 for r in range(R):
                     transpose_x(r)
                     if r >= 1:
@@ -261,4 +271,5 @@ def tile_multilayerallreduce_pa_kernel(tc, x, w_first, w_second, out):
                 evac_red()
             if i == RED_AT + 1:
                 quant_red()
-        evac_out(closed_by(n_items - 1))
+        for i in range(n_items - EV_LAG, n_items):
+            evac_out(closed_by(i))

@@ -17,13 +17,12 @@ W = 1024
 N_CHUNKS = 16
 LAST = N_CHUNKS - 1
 Q_COLS = 256
-RAW_BUFS = 8
+RAW_BUFS = 7
 GRP_BUFS = 4
 CODE_BUFS = 6
 LATE = 5
 X_AFTER = 1
 RED_AT = 9
-EV_LAG = 2
 XV = ()
 
 FLOPS = 2 * 2 * R * T * H * F
@@ -77,10 +76,22 @@ def tile_multilayerallreduce_pa_kernel(tc, x, w_first, w_second, out):
 
         def load_w(c):
             r, g = (c % 8) // 2, c % 2
-            t = rawp.tile([P, PACK, W], BF16, name="raw%d" % c, tag="raw")
             rows = (w_first if c < 8 else w_second)[r, g * K_PASS : (g + 1) * K_PASS, :]
-            nc.sync.dma_start(out=t[:], in_=rows.rearrange("(p j) f -> p j f", j=PACK))
-            raw[c] = t
+            rows = rows.rearrange("(p j) f -> p j f", j=PACK)
+            raw[c] = []
+            if c < LAST:
+                t = rawp.tile([P, PACK, W], BF16, name="raw%d" % c, tag="raw")
+                nc.sync.dma_start(out=t[:], in_=rows)
+                raw[c].append((0, t))
+            else:
+                for col0 in (0, W // 2):
+                    t = rawp.tile([P, PACK, W // 2], BF16, name="raw%d_%d" % (c, col0), tag="rawhalf", bufs=2)
+                    nc.sync.dma_start(out=t[:], in_=rows[:, :, col0 : col0 + W // 2])
+                    raw[c].append((col0, t))
+
+        def raw_cols(c, col0, cols):
+            first, t = [(first, t) for first, t in raw[c] if first <= col0][-1]
+            return t[:, :, col0 - first : col0 - first + cols]
 
         for c in range(X_AFTER + 1):
             load_w(c)
@@ -132,7 +143,7 @@ def tile_multilayerallreduce_pa_kernel(tc, x, w_first, w_second, out):
                     dst = dst.rearrange("p (i q) t -> p q t i", i=4)
                 else:
                     dst = dst.rearrange("p (q i) t -> p q t i", i=4)
-                eng_copy(out=dst, in_=raw[c][:, :, col0 : col0 + cols].rearrange("p t (q i) -> p q t i", i=4))
+                eng_copy(out=dst, in_=raw_cols(c, col0, cols).rearrange("p t (q i) -> p q t i", i=4))
                 at += cols
             grp[i] = g
 
@@ -249,16 +260,16 @@ def tile_multilayerallreduce_pa_kernel(tc, x, w_first, w_second, out):
                     in_=ot[:],
                 )
 
+        due = {}
         for i in range(n_items):
             regroup(i)
             if i + RAW_BUFS < N_CHUNKS:
                 load_w(i + RAW_BUFS)
-            if i == RED_AT + 1:
-                regroup_red()
-            evac_out(closed_by(i - EV_LAG))
+            evac_out(due.get(i, []))
             quant(i - 1)
             if closed_by(i):
                 quant(i)
+                due[i + (1 if len(closed_by(i)) == 2 else 2)] = closed_by(i)
             if i == X_AFTER:
                 quant(i)
                 for r in range(R):
@@ -270,6 +281,7 @@ def tile_multilayerallreduce_pa_kernel(tc, x, w_first, w_second, out):
             if i == RED_AT:
                 evac_red()
             if i == RED_AT + 1:
+                regroup_red()
                 quant_red()
-        for i in range(n_items - EV_LAG, n_items):
-            evac_out(closed_by(i))
+        for i in range(n_items, n_items + 2):
+            evac_out(due.get(i, []))

@@ -24,6 +24,7 @@ LATE = 5
 X_AFTER = 1
 RED_AT = 9
 XV = ()
+V_OF_16 = 7
 
 FLOPS = 2 * 2 * R * T * H * F
 
@@ -82,16 +83,29 @@ def tile_multilayerallreduce_pa_kernel(tc, x, w_first, w_second, out):
             if c < LAST:
                 t = rawp.tile([P, PACK, W], BF16, name="raw%d" % c, tag="raw")
                 nc.sync.dma_start(out=t[:], in_=rows)
-                raw[c].append((0, t))
+                raw[c].append((0, W, t))
             else:
                 for col0 in (0, W // 2):
                     t = rawp.tile([P, PACK, W // 2], BF16, name="raw%d_%d" % (c, col0), tag="rawhalf", bufs=2)
                     nc.sync.dma_start(out=t[:], in_=rows[:, :, col0 : col0 + W // 2])
-                    raw[c].append((col0, t))
+                    raw[c].append((col0, W // 2, t))
 
         def raw_cols(c, col0, cols):
-            first, t = [(first, t) for first, t in raw[c] if first <= col0][-1]
+            first, t = [(first, t) for first, n, t in raw[c] if first <= col0][-1]
             return t[:, :, col0 - first : col0 - first + cols]
+
+        def parts(i, lo, hi):
+            found = []
+            at = 0
+            for c, col0, cols in items[i]:
+                for first, n, t in raw[c]:
+                    s = max(lo, at + max(first - col0, 0))
+                    e = min(hi, at + min(first + n - col0, cols))
+                    if s < e:
+                        src0 = col0 + (s - at) - first
+                        found.append((s, e - s, t[:, :, src0 : src0 + e - s]))
+                at += cols
+            return found
 
         for c in range(X_AFTER + 1):
             load_w(c)
@@ -136,6 +150,17 @@ def tile_multilayerallreduce_pa_kernel(tc, x, w_first, w_second, out):
 
         def regroup(i):
             g = grpp.tile([P, width(i), PACK], BF16, name="grp%d" % i, tag="grp%d" % width(i), align_bytes=64)
+            if items[i][0][0] >= 8:
+                w = width(i)
+                a = V_OF_16 * w // 16
+                for lo, hi, eng_copy in ((0, a, nc.vector.tensor_copy), (a, w, nc.scalar.copy)):
+                    for s, n, src in parts(i, lo, hi):
+                        eng_copy(
+                            out=g[:, s : s + n, :].rearrange("p (q i) t -> p q t i", i=4),
+                            in_=src.rearrange("p t (q i) -> p q t i", i=4),
+                        )
+                grp[i] = g
+                return
             at = 0
             for (c, col0, cols), eng_copy in zip(shares(i), (nc.vector.tensor_copy, nc.scalar.copy)):
                 dst = g[:, at : at + cols, :]

@@ -21,10 +21,10 @@ RAW_BUFS = 7
 GRP_BUFS = 4
 CODE_BUFS = 6
 LATE = 5
-X_AFTER = 1
+X_AFTER = 3
 RED_AT = 9
-XV = ()
-V_OF_16 = 7
+XV = (1, 5)
+V_OF_32 = 15
 
 FLOPS = 2 * 2 * R * T * H * F
 
@@ -152,7 +152,7 @@ def tile_multilayerallreduce_pa_kernel(tc, x, w_first, w_second, out):
             g = grpp.tile([P, width(i), PACK], BF16, name="grp%d" % i, tag="grp%d" % width(i), align_bytes=64)
             if items[i][0][0] >= 8:
                 w = width(i)
-                a = V_OF_16 * w // 16
+                a = V_OF_32 * w // 32
                 for lo, hi, eng_copy in ((0, a, nc.vector.tensor_copy), (a, w, nc.scalar.copy)):
                     for s, n, src in parts(i, lo, hi):
                         eng_copy(

@@ -17,8 +17,8 @@ W = 1024
 N_CHUNKS = 16
 LAST = N_CHUNKS - 1
 Q_COLS = 256
-RAW_BUFS = 7
-GRP_BUFS = 4
+RAW_BUFS = 5
+GRP_BUFS = 3
 CODE_BUFS = 6
 LATE = 5
 X_AFTER = 3
@@ -75,20 +75,18 @@ def tile_multilayerallreduce_pa_kernel(tc, x, w_first, w_second, out):
             nc.sync.dma_start(out=xr[:], in_=x[r].rearrange("(p tt) h -> p tt h", tt=2))
             xraw.append(xr)
 
-        def load_w(c):
+        def load_w(c, col0=0):
             r, g = (c % 8) // 2, c % 2
             rows = (w_first if c < 8 else w_second)[r, g * K_PASS : (g + 1) * K_PASS, :]
             rows = rows.rearrange("(p j) f -> p j f", j=PACK)
-            raw[c] = []
-            if c < LAST:
+            if c < N_CHUNKS - LATE:
                 t = rawp.tile([P, PACK, W], BF16, name="raw%d" % c, tag="raw")
                 nc.sync.dma_start(out=t[:], in_=rows)
-                raw[c].append((0, W, t))
+                raw[c] = [(0, W, t)]
             else:
-                for col0 in (0, W // 2):
-                    t = rawp.tile([P, PACK, W // 2], BF16, name="raw%d_%d" % (c, col0), tag="rawhalf", bufs=2)
-                    nc.sync.dma_start(out=t[:], in_=rows[:, :, col0 : col0 + W // 2])
-                    raw[c].append((col0, W // 2, t))
+                t = rawp.tile([P, PACK, W // 2], BF16, name="raw%d_%d" % (c, col0), tag="rawhalf", bufs=2 * LATE)
+                nc.sync.dma_start(out=t[:], in_=rows[:, :, col0 : col0 + W // 2])
+                raw.setdefault(c, []).append((col0, W // 2, t))
 
         def raw_cols(c, col0, cols):
             first, t = [(first, t) for first, n, t in raw[c] if first <= col0][-1]
@@ -288,8 +286,12 @@ def tile_multilayerallreduce_pa_kernel(tc, x, w_first, w_second, out):
         due = {}
         for i in range(n_items):
             regroup(i)
-            if i + RAW_BUFS < N_CHUNKS:
+            if i + RAW_BUFS < N_CHUNKS - LATE:
                 load_w(i + RAW_BUFS)
+            if i + RAW_BUFS == N_CHUNKS - LATE - 1:
+                for col0 in (0, W // 2):
+                    for c in range(N_CHUNKS - LATE, N_CHUNKS):
+                        load_w(c, col0)
             evac_out(due.get(i, []))
             quant(i - 1)
             if closed_by(i):

@@ -17,10 +17,14 @@ W = 1024
 N_CHUNKS = 16
 LAST = N_CHUNKS - 1
 Q_COLS = 256
+E_COLS = 128
+BLOCKS = ((0, 512), (512, 256), (768, 128), (896, 128))
+NARROW_BUFS = 3
 RAW_BUFS = 5
+SPLIT = 4
 GRP_BUFS = 3
 CODE_BUFS = 6
-LATE = 5
+LATE = 7
 X_AFTER = 3
 RED_AT = 9
 XV = (1, 5)
@@ -43,9 +47,15 @@ def tile_multilayerallreduce_pa_kernel(tc, x, w_first, w_second, out):
         late = list(range(N_CHUNKS - LATE, LAST))
         items = [[(c, 0, W)] for c in range(N_CHUNKS - LATE)]
         items += [[(c, 0, W // 2)] for c in late + [LAST]]
-        for q in (2, 3):
-            items += [[(late[k], q * Q_COLS, Q_COLS), (late[k + 1], q * Q_COLS, Q_COLS)] for k in range(0, len(late), 2)]
-            items.append([(LAST, q * Q_COLS, Q_COLS)])
+        items += [[(late[k], 2 * Q_COLS, Q_COLS), (late[k + 1], 2 * Q_COLS, Q_COLS)] for k in range(0, len(late), 2)]
+        items.append([(LAST, 2 * Q_COLS, Q_COLS)])
+        for e in (6, 7):
+            for k in range(0, len(late), 4):
+                if len(late) - k >= 4:
+                    items.append([(c, e * E_COLS, E_COLS) for c in late[k : k + 4]])
+                else:
+                    items.append([(c, e * E_COLS, E_COLS) for c in late[k:]])
+            items.append([(LAST, e * E_COLS, E_COLS)])
         n_items = len(items)
 
         def width(i):
@@ -61,7 +71,7 @@ def tile_multilayerallreduce_pa_kernel(tc, x, w_first, w_second, out):
             if i < 0 or items[i][0][0] != LAST:
                 return []
             c, col0, cols = items[i][0]
-            return list(range(col0 // Q_COLS, (col0 + cols) // Q_COLS))
+            return [(b0, bn) for b0, bn in BLOCKS if col0 <= b0 and b0 + bn <= col0 + cols]
 
         raw = {}
         grp = {}
@@ -79,12 +89,12 @@ def tile_multilayerallreduce_pa_kernel(tc, x, w_first, w_second, out):
             r, g = (c % 8) // 2, c % 2
             rows = (w_first if c < 8 else w_second)[r, g * K_PASS : (g + 1) * K_PASS, :]
             rows = rows.rearrange("(p j) f -> p j f", j=PACK)
-            if c < N_CHUNKS - LATE:
+            if c < N_CHUNKS - SPLIT:
                 t = rawp.tile([P, PACK, W], BF16, name="raw%d" % c, tag="raw")
                 nc.sync.dma_start(out=t[:], in_=rows)
                 raw[c] = [(0, W, t)]
             else:
-                t = rawp.tile([P, PACK, W // 2], BF16, name="raw%d_%d" % (c, col0), tag="rawhalf", bufs=2 * LATE)
+                t = rawp.tile([P, PACK, W // 2], BF16, name="raw%d_%d" % (c, col0), tag="rawhalf", bufs=2 * SPLIT)
                 nc.sync.dma_start(out=t[:], in_=rows[:, :, col0 : col0 + W // 2])
                 raw.setdefault(c, []).append((col0, W // 2, t))
 
@@ -147,10 +157,17 @@ def tile_multilayerallreduce_pa_kernel(tc, x, w_first, w_second, out):
             xscales.append(xs)
 
         def regroup(i):
-            g = grpp.tile([P, width(i), PACK], BF16, name="grp%d" % i, tag="grp%d" % width(i), align_bytes=64)
+            g = grpp.tile(
+                [P, width(i), PACK],
+                BF16,
+                name="grp%d" % i,
+                tag="grp%d" % width(i),
+                bufs=(NARROW_BUFS if width(i) <= Q_COLS else GRP_BUFS),
+                align_bytes=64,
+            )
             if items[i][0][0] >= 8:
                 w = width(i)
-                a = V_OF_32 * w // 32
+                a = V_OF_32 * w // 32 // 8 * 8 if len(items[i]) < 4 else w // 2
                 for lo, hi, eng_copy in ((0, a, nc.vector.tensor_copy), (a, w, nc.scalar.copy)):
                     for s, n, src in parts(i, lo, hi):
                         eng_copy(
@@ -196,22 +213,23 @@ def tile_multilayerallreduce_pa_kernel(tc, x, w_first, w_second, out):
 
         def mm2(i):
             if not o:
-                for tt in range(2):
-                    for q in range(W // Q_COLS):
-                        o[(tt, q)] = psum.tile([P, Q_COLS], F32, name="o%d_%d" % (tt, q), tag="bank%d" % (2 * q + tt))
+                for k, (b0, bn) in enumerate(BLOCKS):
+                    for tt in range(2):
+                        o[(tt, b0)] = psum.tile([P, bn], F32, name="o%d_%d" % (tt, b0), tag="bank%d" % (2 * k + tt))
             at = 0
             for c, col0, cols in items[i]:
-                for tt in range(2):
-                    for k in range(cols // Q_COLS):
-                        nc.tensor.matmul_mx(
-                            out=o[(tt, col0 // Q_COLS + k)][:],
-                            lhsT=c2[c % 2][:, tt * P : (tt + 1) * P].bitcast(FP8X4),
-                            lhsT_scale=s2[c % 2][:, tt * P : (tt + 1) * P],
-                            rhs=codes[i][:, at + k * Q_COLS : at + (k + 1) * Q_COLS].bitcast(FP8X4),
-                            rhs_scale=scales[i][:, at + k * Q_COLS : at + (k + 1) * Q_COLS],
-                            start=(c == 8),
-                            stop=(c == LAST),
-                        )
+                for b0, bn in BLOCKS:
+                    if col0 <= b0 and b0 + bn <= col0 + cols:
+                        for tt in range(2):
+                            nc.tensor.matmul_mx(
+                                out=o[(tt, b0)][:],
+                                lhsT=c2[c % 2][:, tt * P : (tt + 1) * P].bitcast(FP8X4),
+                                lhsT_scale=s2[c % 2][:, tt * P : (tt + 1) * P],
+                                rhs=codes[i][:, at + b0 - col0 : at + b0 - col0 + bn].bitcast(FP8X4),
+                                rhs_scale=scales[i][:, at + b0 - col0 : at + b0 - col0 + bn],
+                                start=(c == 8),
+                                stop=(c == LAST),
+                            )
                 at += cols
 
         waiting = []
@@ -228,8 +246,9 @@ def tile_multilayerallreduce_pa_kernel(tc, x, w_first, w_second, out):
         def quant(i):
             if i < 0 or i in codes:
                 return
-            cd = codp.tile([P, width(i)], U32, name="codes%d" % i, tag="codes%d" % width(i), align_bytes=64)
-            sc = codp.tile([P, width(i)], U8, name="scales%d" % i, tag="scales%d" % width(i), align_bytes=64)
+            nb = NARROW_BUFS if width(i) <= Q_COLS else CODE_BUFS
+            cd = codp.tile([P, width(i)], U32, name="codes%d" % i, tag="codes%d" % width(i), bufs=nb, align_bytes=64)
+            sc = codp.tile([P, width(i)], U8, name="scales%d" % i, tag="scales%d" % width(i), bufs=nb, align_bytes=64)
             nc.vector.quantize_mx(
                 out=cd[:].bitcast(FP8X4),
                 scales=sc[:],
@@ -269,34 +288,31 @@ def tile_multilayerallreduce_pa_kernel(tc, x, w_first, w_second, out):
                 s2.append(sc)
             multiply_what_is_ready()
 
-        def evac_out(quarters):
-            if not quarters:
-                return
-            n = len(quarters)
-            ot = keep.tile([P, 2, n * Q_COLS], F32, name="ot%d" % quarters[0])
-            for k, q in enumerate(quarters):
-                nc.vector.tensor_copy(out=ot[:, 0, k * Q_COLS : (k + 1) * Q_COLS], in_=o[(0, q)][:])
-                nc.scalar.copy(out=ot[:, 1, k * Q_COLS : (k + 1) * Q_COLS], in_=o[(1, q)][:])
-            for r in range(R):
-                nc.sync.dma_start(
-                    out=out[r].rearrange("(p tt) h -> p tt h", tt=2)[:, :, quarters[0] * Q_COLS : (quarters[0] + n) * Q_COLS],
-                    in_=ot[:],
-                )
+        def evac_out(blocks):
+            for b0, bn in blocks:
+                ot = keep.tile([P, 2, bn], F32, name="ot%d" % b0)
+                nc.vector.tensor_copy(out=ot[:, 0, :], in_=o[(0, b0)][:])
+                nc.scalar.copy(out=ot[:, 1, :], in_=o[(1, b0)][:])
+                for r in range(R):
+                    nc.sync.dma_start(
+                        out=out[r].rearrange("(p tt) h -> p tt h", tt=2)[:, :, b0 : b0 + bn],
+                        in_=ot[:],
+                    )
 
         due = {}
         for i in range(n_items):
             regroup(i)
-            if i + RAW_BUFS < N_CHUNKS - LATE:
+            if i + RAW_BUFS < N_CHUNKS - SPLIT:
                 load_w(i + RAW_BUFS)
-            if i + RAW_BUFS == N_CHUNKS - LATE - 1:
+            if i + RAW_BUFS == N_CHUNKS - SPLIT - 1:
                 for col0 in (0, W // 2):
-                    for c in range(N_CHUNKS - LATE, N_CHUNKS):
+                    for c in range(N_CHUNKS - SPLIT, N_CHUNKS):
                         load_w(c, col0)
             evac_out(due.get(i, []))
             quant(i - 1)
             if closed_by(i):
                 quant(i)
-                due[i + (1 if len(closed_by(i)) == 2 else 2)] = closed_by(i)
+                due[i + (1 if closed_by(i)[0][0] == 0 else 2)] = closed_by(i)
             if i == X_AFTER:
                 quant(i)
                 for r in range(R):

@@ -28,6 +28,7 @@ LATE = 7
 X_AFTER = 3
 RED_AT = 9
 XV = (1, 5)
+NEIGH = 8
 V_OF_32 = 15
 
 FLOPS = 2 * 2 * R * T * H * F
@@ -167,12 +168,12 @@ def tile_multilayerallreduce_pa_kernel(tc, x, w_first, w_second, out):
             )
             if items[i][0][0] >= 8:
                 w = width(i)
-                a = V_OF_32 * w // 32 // 8 * 8 if len(items[i]) < 4 else w // 2
+                a = V_OF_32 * w // 32 // (2 * NEIGH) * (2 * NEIGH) if len(items[i]) < 4 else w // 2
                 for lo, hi, eng_copy in ((0, a, nc.vector.tensor_copy), (a, w, nc.scalar.copy)):
                     for s, n, src in parts(i, lo, hi):
                         eng_copy(
-                            out=g[:, s : s + n, :].rearrange("p (q i) t -> p q t i", i=4),
-                            in_=src.rearrange("p t (q i) -> p q t i", i=4),
+                            out=g[:, s : s + n, :].rearrange("p (q i) t -> p q t i", i=NEIGH),
+                            in_=src.rearrange("p t (q i) -> p q t i", i=NEIGH),
                         )
                 grp[i] = g
                 return

@@ -294,10 +294,10 @@ def tile_multilayerallreduce_pa_kernel(tc, x, w_first, w_second, out):
                 ot = keep.tile([P, 2, bn], F32, name="ot%d" % b0)
                 nc.vector.tensor_copy(out=ot[:, 0, :], in_=o[(0, b0)][:])
                 nc.scalar.copy(out=ot[:, 1, :], in_=o[(1, b0)][:])
-                for r in range(R):
+                for tt in range(2):
                     nc.sync.dma_start(
-                        out=out[r].rearrange("(p tt) h -> p tt h", tt=2)[:, :, b0 : b0 + bn],
-                        in_=ot[:],
+                        out=out.rearrange("r (p tt) h -> p tt r h", tt=2)[:, tt, :, b0 : b0 + bn],
+                        in_=ot[:, tt, :].unsqueeze(1).to_broadcast([P, R, bn]),
                     )
 
         due = {}

@@ -29,7 +29,7 @@ X_AFTER = 3
 RED_AT = 9
 XV = (1, 5)
 NEIGH = 8
-V_OF_32 = 15
+V_OF_32 = 17
 
 FLOPS = 2 * 2 * R * T * H * F
 

from contextlib import ExitStack

import concourse.mybir as mybir
from concourse.masks import make_identity

F32 = mybir.dt.float32
BF16 = mybir.dt.bfloat16
U32 = mybir.dt.uint32
U8 = mybir.dt.uint8
FP8X4 = mybir.dt.float8_e4m3fn_x4

P = 128
PACK = 4
K_PASS = P * PACK
R, T, H, F = 4, 256, 1024, 1024
W = 1024
N_CHUNKS = 16
LAST = N_CHUNKS - 1
Q_COLS = 256
E_COLS = 128
BLOCKS = ((0, 512), (512, 256), (768, 128), (896, 128))
NARROW_BUFS = 3
RAW_BUFS = 5
SPLIT = 4
GRP_BUFS = 3
CODE_BUFS = 6
LATE = 7
X_AFTER = 3
RED_AT = 9
XV = (1, 5)
NEIGH = 8
V_OF_32 = 17

FLOPS = 2 * 2 * R * T * H * F


def tile_multilayerallreduce_pa_kernel(tc, x, w_first, w_second, out):
    nc = tc.nc
    with ExitStack() as ctx:
        const = ctx.enter_context(tc.tile_pool(name="const", bufs=1))
        keep = ctx.enter_context(tc.tile_pool(name="keep", bufs=1))
        rawp = ctx.enter_context(tc.tile_pool(name="rawp", bufs=RAW_BUFS))
        grpp = ctx.enter_context(tc.tile_pool(name="grpp", bufs=GRP_BUFS))
        codp = ctx.enter_context(tc.tile_pool(name="codp", bufs=CODE_BUFS))
        psum = ctx.enter_context(tc.psum_pool(name="psum", bufs=1))
        ctx.enter_context(tc.manual_schedule())

        late = list(range(N_CHUNKS - LATE, LAST))
        items = [[(c, 0, W)] for c in range(N_CHUNKS - LATE)]
        items += [[(c, 0, W // 2)] for c in late + [LAST]]
        items += [[(late[k], 2 * Q_COLS, Q_COLS), (late[k + 1], 2 * Q_COLS, Q_COLS)] for k in range(0, len(late), 2)]
        items.append([(LAST, 2 * Q_COLS, Q_COLS)])
        for e in (6, 7):
            for k in range(0, len(late), 4):
                if len(late) - k >= 4:
                    items.append([(c, e * E_COLS, E_COLS) for c in late[k : k + 4]])
                else:
                    items.append([(c, e * E_COLS, E_COLS) for c in late[k:]])
            items.append([(LAST, e * E_COLS, E_COLS)])
        n_items = len(items)

        def width(i):
            return sum(cols for c, col0, cols in items[i])

        def shares(i):
            if len(items[i]) == 2:
                return items[i]
            c, col0, cols = items[i][0]
            return [(c, col0, cols // 2), (c, col0 + cols // 2, cols // 2)]

        def closed_by(i):
            if i < 0 or items[i][0][0] != LAST:
                return []
            c, col0, cols = items[i][0]
            return [(b0, bn) for b0, bn in BLOCKS if col0 <= b0 and b0 + bn <= col0 + cols]

        raw = {}
        grp = {}
        codes = {}
        scales = {}

        xraw = []

        def load_x(r):
            xr = keep.tile([P, 2, H], BF16, name="xraw%d" % r)
            nc.sync.dma_start(out=xr[:], in_=x[r].rearrange("(p tt) h -> p tt h", tt=2))
            xraw.append(xr)

        def load_w(c, col0=0):
            r, g = (c % 8) // 2, c % 2
            rows = (w_first if c < 8 else w_second)[r, g * K_PASS : (g + 1) * K_PASS, :]
            rows = rows.rearrange("(p j) f -> p j f", j=PACK)
            if c < N_CHUNKS - SPLIT:
                t = rawp.tile([P, PACK, W], BF16, name="raw%d" % c, tag="raw")
                nc.sync.dma_start(out=t[:], in_=rows)
                raw[c] = [(0, W, t)]
            else:
                t = rawp.tile([P, PACK, W // 2], BF16, name="raw%d_%d" % (c, col0), tag="rawhalf", bufs=2 * SPLIT)
                nc.sync.dma_start(out=t[:], in_=rows[:, :, col0 : col0 + W // 2])
                raw.setdefault(c, []).append((col0, W // 2, t))

        def raw_cols(c, col0, cols):
            first, t = [(first, t) for first, n, t in raw[c] if first <= col0][-1]
            return t[:, :, col0 - first : col0 - first + cols]

        def parts(i, lo, hi):
            found = []
            at = 0
            for c, col0, cols in items[i]:
                for first, n, t in raw[c]:
                    s = max(lo, at + max(first - col0, 0))
                    e = min(hi, at + min(first + n - col0, cols))
                    if s < e:
                        src0 = col0 + (s - at) - first
                        found.append((s, e - s, t[:, :, src0 : src0 + e - s]))
                at += cols
            return found

        for c in range(X_AFTER + 1):
            load_w(c)
        for r in range(R):
            load_x(r)
        for c in range(X_AFTER + 1, RAW_BUFS):
            load_w(c)

        ident = const.tile([P, P], F32, name="ident")
        make_identity(nc, ident[:])

        xcodes = []
        xscales = []
        xgrp = []

        def transpose_x(r):
            xw = xraw[r][:].bitcast(F32)
            gx = keep.tile([P, 2, T, 2], F32, name="gx%d" % r, align_bytes=64)
            for g in range(2):
                xt = psum.tile([P, 2, T], F32, name="xt%d_%d" % (r, g), tag="bank%d" % (2 * r + g))
                for u in range(2):
                    for tt in range(2):
                        nc.tensor.transpose(
                            xt[:, u, tt * P : (tt + 1) * P],
                            xw[:, tt, 256 * g + u : 256 * (g + 1) : 2],
                            ident[:],
                        )
                eng_copy = nc.vector.tensor_copy if 2 * r + g in XV else nc.scalar.copy
                eng_copy(out=gx[:, g, :, :], in_=xt[:].rearrange("p u c -> p c u"))
            xgrp.append(gx)

        def quant_x(r):
            xc = keep.tile([P, 2 * T], U32, name="xc%d" % r, align_bytes=64)
            xs = keep.tile([P, 2 * T], U8, name="xs%d" % r, align_bytes=64)
            nc.vector.quantize_mx(
                out=xc[:].bitcast(FP8X4),
                scales=xs[:],
                in_=xgrp[r][:].rearrange("p g c u -> p (g c u)").bitcast(BF16),
            )
            xcodes.append(xc)
            xscales.append(xs)

        def regroup(i):
            g = grpp.tile(
                [P, width(i), PACK],
                BF16,
                name="grp%d" % i,
                tag="grp%d" % width(i),
                bufs=(NARROW_BUFS if width(i) <= Q_COLS else GRP_BUFS),
                align_bytes=64,
            )
            if items[i][0][0] >= 8:
                w = width(i)
                a = V_OF_32 * w // 32 // (2 * NEIGH) * (2 * NEIGH) if len(items[i]) < 4 else w // 2
                for lo, hi, eng_copy in ((0, a, nc.vector.tensor_copy), (a, w, nc.scalar.copy)):
                    for s, n, src in parts(i, lo, hi):
                        eng_copy(
                            out=g[:, s : s + n, :].rearrange("p (q i) t -> p q t i", i=NEIGH),
                            in_=src.rearrange("p t (q i) -> p q t i", i=NEIGH),
                        )
                grp[i] = g
                return
            at = 0
            for (c, col0, cols), eng_copy in zip(shares(i), (nc.vector.tensor_copy, nc.scalar.copy)):
                dst = g[:, at : at + cols, :]
                if c < 8:
                    dst = dst.rearrange("p (i q) t -> p q t i", i=4)
                else:
                    dst = dst.rearrange("p (q i) t -> p q t i", i=4)
                eng_copy(out=dst, in_=raw_cols(c, col0, cols).rearrange("p t (q i) -> p q t i", i=4))
                at += cols
            grp[i] = g

        y = []
        o = {}
        red = []
        g2 = []
        c2 = []
        s2 = []

        def mm1(i):
            c = items[i][0][0]
            r, g = c // 2, c % 2
            if c == 0:
                for m in range(8):
                    y.append(psum.tile([P, T], F32, name="y%d" % m, tag="bank%d" % m))
            for m in range(8):
                nc.tensor.matmul_mx(
                    out=y[m][:],
                    lhsT=codes[i][:, m * P : (m + 1) * P].bitcast(FP8X4),
                    lhsT_scale=scales[i][:, m * P : (m + 1) * P],
                    rhs=xcodes[r][:, g * T : (g + 1) * T].bitcast(FP8X4),
                    rhs_scale=xscales[r][:, g * T : (g + 1) * T],
                    start=(c == 0),
                    stop=(c == 7),
                )

        def mm2(i):
            if not o:
                for k, (b0, bn) in enumerate(BLOCKS):
                    for tt in range(2):
                        o[(tt, b0)] = psum.tile([P, bn], F32, name="o%d_%d" % (tt, b0), tag="bank%d" % (2 * k + tt))
            at = 0
            for c, col0, cols in items[i]:
                for b0, bn in BLOCKS:
                    if col0 <= b0 and b0 + bn <= col0 + cols:
                        for tt in range(2):
                            nc.tensor.matmul_mx(
                                out=o[(tt, b0)][:],
                                lhsT=c2[c % 2][:, tt * P : (tt + 1) * P].bitcast(FP8X4),
                                lhsT_scale=s2[c % 2][:, tt * P : (tt + 1) * P],
                                rhs=codes[i][:, at + b0 - col0 : at + b0 - col0 + bn].bitcast(FP8X4),
                                rhs_scale=scales[i][:, at + b0 - col0 : at + b0 - col0 + bn],
                                start=(c == 8),
                                stop=(c == LAST),
                            )
                at += cols

        waiting = []
        multiplied = set()

        def multiply_what_is_ready():
            for i in waiting:
                first_layer = items[i][0][0] < 8
                ready = len(xcodes) == R if first_layer else len(c2) == 2
                if ready and i not in multiplied:
                    (mm1 if first_layer else mm2)(i)
                    multiplied.add(i)

        def quant(i):
            if i < 0 or i in codes:
                return
            nb = NARROW_BUFS if width(i) <= Q_COLS else CODE_BUFS
            cd = codp.tile([P, width(i)], U32, name="codes%d" % i, tag="codes%d" % width(i), bufs=nb, align_bytes=64)
            sc = codp.tile([P, width(i)], U8, name="scales%d" % i, tag="scales%d" % width(i), bufs=nb, align_bytes=64)
            nc.vector.quantize_mx(
                out=cd[:].bitcast(FP8X4),
                scales=sc[:],
                in_=grp[i][:].rearrange("p w t -> p (w t)"),
            )
            codes[i] = cd
            scales[i] = sc
            waiting.append(i)
            multiply_what_is_ready()

        def evac_red():
            for g in range(2):
                rp = keep.tile([P, PACK, T], BF16, name="red%d" % g)
                for t in range(PACK):
                    nc.scalar.copy(out=rp[:, t, :], in_=y[PACK * g + t][:])
                red.append(rp)

        def regroup_red():
            for g in range(2):
                gg = keep.tile([P, T, PACK], BF16, name="g2_%d" % g, align_bytes=64)
                nc.vector.tensor_copy(
                    out=gg[:].rearrange("p (q i) t -> p q t i", i=4),
                    in_=red[g][:].rearrange("p t (q i) -> p q t i", i=4),
                )
                g2.append(gg)

        def quant_red():
            for g in range(2):
                cd = keep.tile([P, T], U32, name="c2_%d" % g, align_bytes=64)
                sc = keep.tile([P, T], U8, name="s2_%d" % g, align_bytes=64)
                nc.vector.quantize_mx(
                    out=cd[:].bitcast(FP8X4),
                    scales=sc[:],
                    in_=g2[g][:].rearrange("p w t -> p (w t)"),
                )
                c2.append(cd)
                s2.append(sc)
            multiply_what_is_ready()

        def evac_out(blocks):
            for b0, bn in blocks:
                ot = keep.tile([P, 2, bn], F32, name="ot%d" % b0)
                nc.vector.tensor_copy(out=ot[:, 0, :], in_=o[(0, b0)][:])
                nc.scalar.copy(out=ot[:, 1, :], in_=o[(1, b0)][:])
                for tt in range(2):
                    nc.sync.dma_start(
                        out=out.rearrange("r (p tt) h -> p tt r h", tt=2)[:, tt, :, b0 : b0 + bn],
                        in_=ot[:, tt, :].unsqueeze(1).to_broadcast([P, R, bn]),
                    )

        due = {}
        for i in range(n_items):
            regroup(i)
            if i + RAW_BUFS < N_CHUNKS - SPLIT:
                load_w(i + RAW_BUFS)
            if i + RAW_BUFS == N_CHUNKS - SPLIT - 1:
                for col0 in (0, W // 2):
                    for c in range(N_CHUNKS - SPLIT, N_CHUNKS):
                        load_w(c, col0)
            evac_out(due.get(i, []))
            quant(i - 1)
            if closed_by(i):
                quant(i)
                due[i + (1 if closed_by(i)[0][0] == 0 else 2)] = closed_by(i)
            if i == X_AFTER:
                quant(i)
                for r in range(R):
                    transpose_x(r)
                    if r >= 1:
                        quant_x(r - 1)
                quant_x(R - 1)
                multiply_what_is_ready()
            if i == RED_AT:
                evac_red()
            if i == RED_AT + 1:
                regroup_red()
                quant_red()
        for i in range(n_items, n_items + 2):
            evac_out(due.get(i, []))
